import numpy as np
import ml_dtypes

BF16 = ml_dtypes.bfloat16


def bf(x):
    return np.asarray(x, np.float32).astype(BF16)


def f32(x):
    return np.asarray(x, np.float32)


def f64(x):
    return np.asarray(x).astype(np.float64)


def striped(idx):
    return np.tile(idx.reshape(-1, 16).T, (8, 1))


E, CTX, PAD, H1, H2, H3, C, S, N = 128, 5, 2, 512, 256, 128, 1024, 4096, 2048


def setup_inputs():
    return {
        "x": bf(np.random.standard_normal((E, N))),
        "w1": bf(np.random.standard_normal((CTX * E, H1)) / np.sqrt(CTX * E)),
        "b1": f32(0.1 * np.random.standard_normal((H1, 1))),
        "w2": bf(np.random.standard_normal((H1, H2)) * np.sqrt(2.0 / H1)),
        "b2": f32(0.1 * np.random.standard_normal((H2, 1))),
        "w3": bf(np.random.standard_normal((H2, H3)) * np.sqrt(2.0 / H2)),
        "b3": f32(0.1 * np.random.standard_normal((H3, 1))),
        "w4": bf(np.random.standard_normal((H3, C)) * np.sqrt(2.0 / H3)),
        "b4": f32(0.1 * np.random.standard_normal((C, 1))),
        "base": f32(np.random.standard_normal((C, S))),
        "offs": striped(np.random.permutation(S)[:N]),
    }


def reference(x, w1, b1, w2, b2, w3, b3, w4, b4, base, offs):
    idx = offs[:16].T.reshape(-1)
    xp = np.pad(f64(x), ((0, 0), (PAD, PAD)))
    ctx = np.concatenate([xp[:, i:i + N] for i in range(CTX)], axis=0)
    h = np.maximum(f64(w1).T @ ctx + f64(b1), 0.0)
    h = np.maximum(f64(w2).T @ h + f64(b2), 0.0)
    h = np.maximum(f64(w3).T @ h + f64(b3), 0.0)
    res = f64(base).copy()
    res[:, idx] = f64(w4).T @ h + f64(b4)
    return res

@@ -1,0 +1,112 @@
+import concourse.mybir as mybir
+
+F32 = mybir.dt.float32
+BF16 = mybir.dt.bfloat16
+U16 = mybir.dt.uint16
+RELU = mybir.ActivationFunctionType.Relu
+ADD = mybir.AluOpType.add
+
+P = 128
+E, CTX, PAD = 128, 5, 2
+H1, H2, H3 = 512, 256, 128
+C, S, N = 1024, 4096, 2048
+BANK = 512
+CHUNKS = N // BANK
+
+FLOPS = 2 * N * (CTX * E * H1 + H1 * H2 + H2 * H3 + H3 * C)
+
+
+def tile_contextualmlpdecryptor_b_kernel(tc, x, w1, b1, w2, b2, w3, b3, w4, b4, base, offs, out):
+    nc = tc.nc
+    with (
+        tc.tile_pool(name="held", bufs=1) as held,
+        tc.tile_pool(name="dense", bufs=3) as dense,
+        tc.tile_pool(name="wide", bufs=2) as wide,
+        tc.psum_pool(name="psum", bufs=8) as psum,
+    ):
+        xp = held.tile([P, N + 2 * PAD], BF16, name="xp")
+        nc.vector.memset(xp[:, 0:16], 0.0)
+        nc.vector.memset(xp[:, N : N + 2 * PAD], 0.0)
+        nc.sync.dma_start(xp[:, PAD : PAD + N], x)
+        w1_sb = held.tile([P, CTX, H1], BF16, name="w1_sb")
+        nc.sync.dma_start(w1_sb[:], w1.rearrange("(i e) m -> e i m", e=E))
+        w2_sb = held.tile([P, H1 // P, H2], BF16, name="w2_sb")
+        nc.sync.dma_start(w2_sb[:], w2.rearrange("(k p) m -> p k m", p=P))
+        w3_sb = held.tile([P, H2 // P, H3], BF16, name="w3_sb")
+        nc.sync.dma_start(w3_sb[:], w3.rearrange("(k p) m -> p k m", p=P))
+        w4_sb = held.tile([P, C], BF16, name="w4_sb")
+        nc.sync.dma_start(w4_sb[:], w4)
+        offsets = held.tile([P, N // 16], U16, name="offsets")
+        nc.sync.dma_start(offsets[:], offs)
+
+        b1_sb = held.tile([P, H1 // P], F32, name="b1_sb")
+        b2_sb = held.tile([P, H2 // P], F32, name="b2_sb")
+        b3_sb = held.tile([P, H3 // P], F32, name="b3_sb")
+        b4_sb = held.tile([P, C // P], F32, name="b4_sb")
+        with nc.allow_non_contiguous_dma(reason="a bias has one 4-byte value for each partition"):
+            for bias_sb, bias in ((b1_sb, b1), (b2_sb, b2), (b3_sb, b3), (b4_sb, b4)):
+                nc.scalar.dma_start(bias_sb[:], bias.rearrange("(m p) o -> p (m o)", p=P))
+
+        windows = [held.tile([P, S], F32, name=f"window{c}") for c in range(C // P)]
+        for c in range(C // P):
+            nc.sync.dma_start(windows[c][:], base[c * P : (c + 1) * P, :])
+
+        def widen_bias(c):
+            b4_wide = wide.tile([P, N], F32, name="b4_wide")
+            nc.scalar.copy(b4_wide[:], b4_sb[:, c : c + 1].to_broadcast([P, N]))
+            return b4_wide
+
+        b4_wide = widen_bias(0)
+
+        h1 = [held.tile([P, H1 // P, BANK], BF16, name=f"h1_{n}") for n in range(CHUNKS)]
+        for n in range(CHUNKS):
+            for m in range(H1 // P):
+                acc = psum.tile([P, BANK], F32, name="acc")
+                for i in range(CTX):
+                    nc.tensor.matmul(
+                        acc[:],
+                        w1_sb[:, i, m * P : (m + 1) * P],
+                        xp[:, n * BANK + i : n * BANK + i + BANK],
+                        start=(i == 0),
+                        stop=(i == CTX - 1),
+                    )
+                nc.scalar.activation(h1[n][:, m, :], acc[:], RELU, bias=b1_sb[:, m : m + 1])
+
+        h2 = [held.tile([P, H2 // P, BANK], BF16, name=f"h2_{n}") for n in range(CHUNKS)]
+        for n in range(CHUNKS):
+            for m in range(H2 // P):
+                acc = psum.tile([P, BANK], F32, name="acc")
+                for k in range(H1 // P):
+                    nc.tensor.matmul(
+                        acc[:],
+                        w2_sb[:, k, m * P : (m + 1) * P],
+                        h1[n][:, k, :],
+                        start=(k == 0),
+                        stop=(k == H1 // P - 1),
+                    )
+                nc.scalar.activation(h2[n][:, m, :], acc[:], RELU, bias=b2_sb[:, m : m + 1])
+
+        h3 = [held.tile([P, BANK], BF16, name=f"h3_{n}") for n in range(CHUNKS)]
+        for n in range(CHUNKS):
+            acc = psum.tile([P, BANK], F32, name="acc")
+            for k in range(H2 // P):
+                nc.tensor.matmul(
+                    acc[:], w3_sb[:, k, :], h2[n][:, k, :], start=(k == 0), stop=(k == H2 // P - 1)
+                )
+            nc.scalar.activation(h3[n][:], acc[:], RELU, bias=b3_sb[:, 0:1])
+
+        for c in range(C // P):
+            product = dense.tile([P, N], F32, name="product")
+            for n in range(CHUNKS):
+                acc = psum.tile([P, BANK], F32, name="acc")
+                nc.tensor.matmul(acc[:], w4_sb[:, c * P : (c + 1) * P], h3[n][:], start=True, stop=True)
+                nc.scalar.copy(product[:, n * BANK : (n + 1) * BANK], acc[:])
+            nc.vector.tensor_tensor(
+                windows[c][:].indirect(offsets[:]),
+                product[:],
+                b4_wide[:],
+                ADD,
+            )
+            nc.sync.dma_start(out[c * P : (c + 1) * P, :], windows[c][:])
+            if c + 1 < C // P:
+                b4_wide = widen_bias(c + 1)

@@ -5,6 +5,7 @@ BF16 = mybir.dt.bfloat16
 U16 = mybir.dt.uint16
 RELU = mybir.ActivationFunctionType.Relu
 ADD = mybir.AluOpType.add
+MAX = mybir.AluOpType.max
 
 P = 128
 E, CTX, PAD = 128, 5, 2
@@ -58,6 +59,12 @@ def tile_contextualmlpdecryptor_b_kernel(tc, x, w1, b1, w2, b2, w3, b3, w4, b4, 
 
         b4_wide = widen_bias(0)
 
+        def relu_bias(turn, out_ap, acc, bias_column):
+            if turn % 2 == 0:
+                nc.scalar.activation(out_ap, acc[:], RELU, bias=bias_column)
+            else:
+                nc.vector.tensor_scalar(out_ap, acc[:], bias_column, 0.0, ADD, MAX)
+
         h1 = [held.tile([P, H1 // P, BANK], BF16, name=f"h1_{n}") for n in range(CHUNKS)]
         for n in range(CHUNKS):
             for m in range(H1 // P):
@@ -70,7 +77,7 @@ def tile_contextualmlpdecryptor_b_kernel(tc, x, w1, b1, w2, b2, w3, b3, w4, b4, 
                         start=(i == 0),
                         stop=(i == CTX - 1),
                     )
-                nc.scalar.activation(h1[n][:, m, :], acc[:], RELU, bias=b1_sb[:, m : m + 1])
+                relu_bias(m, h1[n][:, m, :], acc, b1_sb[:, m : m + 1])
 
         h2 = [held.tile([P, H2 // P, BANK], BF16, name=f"h2_{n}") for n in range(CHUNKS)]
         for n in range(CHUNKS):
@@ -84,7 +91,7 @@ def tile_contextualmlpdecryptor_b_kernel(tc, x, w1, b1, w2, b2, w3, b3, w4, b4, 
                         start=(k == 0),
                         stop=(k == H1 // P - 1),
                     )
-                nc.scalar.activation(h2[n][:, m, :], acc[:], RELU, bias=b2_sb[:, m : m + 1])
+                relu_bias(m, h2[n][:, m, :], acc, b2_sb[:, m : m + 1])
 
         h3 = [held.tile([P, BANK], BF16, name=f"h3_{n}") for n in range(CHUNKS)]
         for n in range(CHUNKS):
@@ -93,14 +100,17 @@ def tile_contextualmlpdecryptor_b_kernel(tc, x, w1, b1, w2, b2, w3, b3, w4, b4, 
                 nc.tensor.matmul(
                     acc[:], w3_sb[:, k, :], h2[n][:, k, :], start=(k == 0), stop=(k == H2 // P - 1)
                 )
-            nc.scalar.activation(h3[n][:], acc[:], RELU, bias=b3_sb[:, 0:1])
+            relu_bias(n, h3[n][:], acc, b3_sb[:, 0:1])
 
         for c in range(C // P):
             product = dense.tile([P, N], F32, name="product")
             for n in range(CHUNKS):
                 acc = psum.tile([P, BANK], F32, name="acc")
                 nc.tensor.matmul(acc[:], w4_sb[:, c * P : (c + 1) * P], h3[n][:], start=True, stop=True)
-                nc.scalar.copy(product[:, n * BANK : (n + 1) * BANK], acc[:])
+                if c == 0 and n % 2 == 1:
+                    nc.vector.tensor_copy(product[:, n * BANK : (n + 1) * BANK], acc[:])
+                else:
+                    nc.scalar.copy(product[:, n * BANK : (n + 1) * BANK], acc[:])
             nc.vector.tensor_tensor(
                 windows[c][:].indirect(offsets[:]),
                 product[:],

@@ -13,6 +13,7 @@ H1, H2, H3 = 512, 256, 128
 C, S, N = 1024, 4096, 2048
 BANK = 512
 CHUNKS = N // BANK
+MARGIN = 16
 
 FLOPS = 2 * N * (CTX * E * H1 + H1 * H2 + H2 * H3 + H3 * C)
 
@@ -25,12 +26,14 @@ def tile_contextualmlpdecryptor_b_kernel(tc, x, w1, b1, w2, b2, w3, b3, w4, b4, 
         tc.tile_pool(name="wide", bufs=2) as wide,
         tc.psum_pool(name="psum", bufs=8) as psum,
     ):
-        xp = held.tile([P, N + 2 * PAD], BF16, name="xp")
-        nc.vector.memset(xp[:, 0:16], 0.0)
-        nc.vector.memset(xp[:, N : N + 2 * PAD], 0.0)
-        nc.sync.dma_start(xp[:, PAD : PAD + N], x)
+        xp = held.tile([P, MARGIN + N + MARGIN], BF16, name="xp")
+        nc.vector.memset(xp[:, 0:MARGIN], 0.0)
+        nc.vector.memset(xp[:, MARGIN + N : MARGIN + N + MARGIN], 0.0)
         w1_sb = held.tile([P, CTX, H1], BF16, name="w1_sb")
-        nc.sync.dma_start(w1_sb[:], w1.rearrange("(i e) m -> e i m", e=E))
+        for n in range(CHUNKS):
+            nc.sync.dma_start(xp[:, MARGIN + n * BANK : MARGIN + (n + 1) * BANK], x[:, n * BANK : (n + 1) * BANK])
+        for i in range(CTX):
+            nc.scalar.dma_start(w1_sb[:, i, :], w1[i * E : (i + 1) * E, :])
         w2_sb = held.tile([P, H1 // P, H2], BF16, name="w2_sb")
         nc.sync.dma_start(w2_sb[:], w2.rearrange("(k p) m -> p k m", p=P))
         w3_sb = held.tile([P, H2 // P, H3], BF16, name="w3_sb")
@@ -73,7 +76,7 @@ def tile_contextualmlpdecryptor_b_kernel(tc, x, w1, b1, w2, b2, w3, b3, w4, b4, 
                     nc.tensor.matmul(
                         acc[:],
                         w1_sb[:, i, m * P : (m + 1) * P],
-                        xp[:, n * BANK + i : n * BANK + i + BANK],
+                        xp[:, MARGIN - PAD + n * BANK + i : MARGIN - PAD + n * BANK + i + BANK],
                         start=(i == 0),
                         stop=(i == CTX - 1),
                     )

@@ -13,6 +13,7 @@ H1, H2, H3 = 512, 256, 128
 C, S, N = 1024, 4096, 2048
 BANK = 512
 CHUNKS = N // BANK
+WARM_UP = 4
 MARGIN = 16
 
 FLOPS = 2 * N * (CTX * E * H1 + H1 * H2 + H2 * H3 + H3 * C)
@@ -26,6 +27,12 @@ def tile_contextualmlpdecryptor_b_kernel(tc, x, w1, b1, w2, b2, w3, b3, w4, b4, 
         tc.tile_pool(name="wide", bufs=2) as wide,
         tc.psum_pool(name="psum", bufs=8) as psum,
     ):
+        zeros = held.tile([P, BANK], BF16, name="zeros")
+        nc.vector.memset(zeros[:], 0.0)
+        unread = psum.tile([P, BANK], F32, name="acc")
+        for turn in range(WARM_UP):
+            nc.tensor.matmul(unread[:], zeros[:, 0:P], zeros[:], start=True, stop=True)
+
         xp = held.tile([P, MARGIN + N + MARGIN], BF16, name="xp")
         nc.vector.memset(xp[:, 0:MARGIN], 0.0)
         nc.vector.memset(xp[:, MARGIN + N : MARGIN + N + MARGIN], 0.0)

@@ -12,8 +12,10 @@ E, CTX, PAD = 128, 5, 2
 H1, H2, H3 = 512, 256, 128
 C, S, N = 1024, 4096, 2048
 BANK = 512
-CHUNKS = N // BANK
-WARM_UP = 4
+WIDTHS = (BANK,) * (N // BANK - 1) + (BANK // 2,) * 2
+STARTS = tuple(sum(WIDTHS[:n]) for n in range(len(WIDTHS)))
+CHUNKS = len(WIDTHS)
+WARM_UP = 2
 MARGIN = 16
 
 FLOPS = 2 * N * (CTX * E * H1 + H1 * H2 + H2 * H3 + H3 * C)
@@ -37,7 +39,7 @@ def tile_contextualmlpdecryptor_b_kernel(tc, x, w1, b1, w2, b2, w3, b3, w4, b4, 
         nc.vector.memset(xp[:, 0:MARGIN], 0.0)
         nc.vector.memset(xp[:, MARGIN + N : MARGIN + N + MARGIN], 0.0)
         w1_sb = held.tile([P, CTX, H1], BF16, name="w1_sb")
-        for n in range(CHUNKS):
+        for n in range(N // BANK):
             nc.sync.dma_start(xp[:, MARGIN + n * BANK : MARGIN + (n + 1) * BANK], x[:, n * BANK : (n + 1) * BANK])
         for i in range(CTX):
             nc.scalar.dma_start(w1_sb[:, i, :], w1[i * E : (i + 1) * E, :])
@@ -71,56 +73,58 @@ def tile_contextualmlpdecryptor_b_kernel(tc, x, w1, b1, w2, b2, w3, b3, w4, b4, 
 
         def relu_bias(turn, out_ap, acc, bias_column):
             if turn % 2 == 0:
-                nc.scalar.activation(out_ap, acc[:], RELU, bias=bias_column)
+                nc.scalar.activation(out_ap, acc, RELU, bias=bias_column)
             else:
-                nc.vector.tensor_scalar(out_ap, acc[:], bias_column, 0.0, ADD, MAX)
+                nc.vector.tensor_scalar(out_ap, acc, bias_column, 0.0, ADD, MAX)
 
-        h1 = [held.tile([P, H1 // P, BANK], BF16, name=f"h1_{n}") for n in range(CHUNKS)]
+        h1 = [held.tile([P, H1 // P, WIDTHS[n]], BF16, name=f"h1_{n}") for n in range(CHUNKS)]
         for n in range(CHUNKS):
             for m in range(H1 // P):
                 acc = psum.tile([P, BANK], F32, name="acc")
                 for i in range(CTX):
                     nc.tensor.matmul(
-                        acc[:],
+                        acc[:, 0 : WIDTHS[n]],
                         w1_sb[:, i, m * P : (m + 1) * P],
-                        xp[:, MARGIN - PAD + n * BANK + i : MARGIN - PAD + n * BANK + i + BANK],
+                        xp[:, MARGIN - PAD + STARTS[n] + i : MARGIN - PAD + STARTS[n] + i + WIDTHS[n]],
                         start=(i == 0),
                         stop=(i == CTX - 1),
                     )
-                relu_bias(m, h1[n][:, m, :], acc, b1_sb[:, m : m + 1])
+                relu_bias(m, h1[n][:, m, :], acc[:, 0 : WIDTHS[n]], b1_sb[:, m : m + 1])
 
-        h2 = [held.tile([P, H2 // P, BANK], BF16, name=f"h2_{n}") for n in range(CHUNKS)]
+        h2 = [held.tile([P, H2 // P, WIDTHS[n]], BF16, name=f"h2_{n}") for n in range(CHUNKS)]
         for n in range(CHUNKS):
             for m in range(H2 // P):
                 acc = psum.tile([P, BANK], F32, name="acc")
                 for k in range(H1 // P):
                     nc.tensor.matmul(
-                        acc[:],
+                        acc[:, 0 : WIDTHS[n]],
                         w2_sb[:, k, m * P : (m + 1) * P],
                         h1[n][:, k, :],
                         start=(k == 0),
                         stop=(k == H1 // P - 1),
                     )
-                relu_bias(m, h2[n][:, m, :], acc, b2_sb[:, m : m + 1])
+                relu_bias(m, h2[n][:, m, :], acc[:, 0 : WIDTHS[n]], b2_sb[:, m : m + 1])
 
-        h3 = [held.tile([P, BANK], BF16, name=f"h3_{n}") for n in range(CHUNKS)]
+        h3 = [held.tile([P, WIDTHS[n]], BF16, name=f"h3_{n}") for n in range(CHUNKS)]
         for n in range(CHUNKS):
             acc = psum.tile([P, BANK], F32, name="acc")
             for k in range(H2 // P):
                 nc.tensor.matmul(
-                    acc[:], w3_sb[:, k, :], h2[n][:, k, :], start=(k == 0), stop=(k == H2 // P - 1)
+                    acc[:, 0 : WIDTHS[n]], w3_sb[:, k, :], h2[n][:, k, :], start=(k == 0), stop=(k == H2 // P - 1)
                 )
-            relu_bias(n, h3[n][:], acc, b3_sb[:, 0:1])
+            relu_bias(n, h3[n][:], acc[:, 0 : WIDTHS[n]], b3_sb[:, 0:1])
 
         for c in range(C // P):
             product = dense.tile([P, N], F32, name="product")
             for n in range(CHUNKS):
                 acc = psum.tile([P, BANK], F32, name="acc")
-                nc.tensor.matmul(acc[:], w4_sb[:, c * P : (c + 1) * P], h3[n][:], start=True, stop=True)
+                nc.tensor.matmul(
+                    acc[:, 0 : WIDTHS[n]], w4_sb[:, c * P : (c + 1) * P], h3[n][:], start=True, stop=True
+                )
                 if c == 0 and n % 2 == 1:
-                    nc.vector.tensor_copy(product[:, n * BANK : (n + 1) * BANK], acc[:])
+                    nc.vector.tensor_copy(product[:, STARTS[n] : STARTS[n] + WIDTHS[n]], acc[:, 0 : WIDTHS[n]])
                 else:
-                    nc.scalar.copy(product[:, n * BANK : (n + 1) * BANK], acc[:])
+                    nc.scalar.copy(product[:, STARTS[n] : STARTS[n] + WIDTHS[n]], acc[:, 0 : WIDTHS[n]])
             nc.vector.tensor_tensor(
                 windows[c][:].indirect(offsets[:]),
                 product[:],

@@ -43,6 +43,13 @@ def tile_contextualmlpdecryptor_b_kernel(tc, x, w1, b1, w2, b2, w3, b3, w4, b4, 
             nc.sync.dma_start(xp[:, MARGIN + n * BANK : MARGIN + (n + 1) * BANK], x[:, n * BANK : (n + 1) * BANK])
         for i in range(CTX):
             nc.scalar.dma_start(w1_sb[:, i, :], w1[i * E : (i + 1) * E, :])
+        b1_sb = held.tile([P, H1 // P], F32, name="b1_sb")
+        b2_sb = held.tile([P, H2 // P], F32, name="b2_sb")
+        b3_sb = held.tile([P, H3 // P], F32, name="b3_sb")
+        b4_sb = held.tile([P, C // P], F32, name="b4_sb")
+        with nc.allow_non_contiguous_dma(reason="a bias has one 4-byte value for each partition"):
+            for bias_sb, bias in ((b1_sb, b1), (b2_sb, b2), (b3_sb, b3), (b4_sb, b4)):
+                nc.sync.dma_start(bias_sb[:], bias.rearrange("(m p) o -> p (m o)", p=P))
         w2_sb = held.tile([P, H1 // P, H2], BF16, name="w2_sb")
         nc.sync.dma_start(w2_sb[:], w2.rearrange("(k p) m -> p k m", p=P))
         w3_sb = held.tile([P, H2 // P, H3], BF16, name="w3_sb")
@@ -51,14 +58,6 @@ def tile_contextualmlpdecryptor_b_kernel(tc, x, w1, b1, w2, b2, w3, b3, w4, b4, 
         nc.sync.dma_start(w4_sb[:], w4)
         offsets = held.tile([P, N // 16], U16, name="offsets")
         nc.sync.dma_start(offsets[:], offs)
-
-        b1_sb = held.tile([P, H1 // P], F32, name="b1_sb")
-        b2_sb = held.tile([P, H2 // P], F32, name="b2_sb")
-        b3_sb = held.tile([P, H3 // P], F32, name="b3_sb")
-        b4_sb = held.tile([P, C // P], F32, name="b4_sb")
-        with nc.allow_non_contiguous_dma(reason="a bias has one 4-byte value for each partition"):
-            for bias_sb, bias in ((b1_sb, b1), (b2_sb, b2), (b3_sb, b3), (b4_sb, b4)):
-                nc.scalar.dma_start(bias_sb[:], bias.rearrange("(m p) o -> p (m o)", p=P))
 
         windows = [held.tile([P, S], F32, name=f"window{c}") for c in range(C // P)]
         for c in range(C // P):

@@ -39,10 +39,11 @@ def tile_contextualmlpdecryptor_b_kernel(tc, x, w1, b1, w2, b2, w3, b3, w4, b4, 
         nc.vector.memset(xp[:, 0:MARGIN], 0.0)
         nc.vector.memset(xp[:, MARGIN + N : MARGIN + N + MARGIN], 0.0)
         w1_sb = held.tile([P, CTX, H1], BF16, name="w1_sb")
-        for n in range(N // BANK):
-            nc.sync.dma_start(xp[:, MARGIN + n * BANK : MARGIN + (n + 1) * BANK], x[:, n * BANK : (n + 1) * BANK])
+        nc.sync.dma_start(xp[:, MARGIN : MARGIN + BANK], x[:, 0:BANK])
         for i in range(CTX):
-            nc.scalar.dma_start(w1_sb[:, i, :], w1[i * E : (i + 1) * E, :])
+            nc.sync.dma_start(w1_sb[:, i, :], w1[i * E : (i + 1) * E, :])
+        for n in range(1, N // BANK):
+            nc.sync.dma_start(xp[:, MARGIN + n * BANK : MARGIN + (n + 1) * BANK], x[:, n * BANK : (n + 1) * BANK])
         b1_sb = held.tile([P, H1 // P], F32, name="b1_sb")
         b2_sb = held.tile([P, H2 // P], F32, name="b2_sb")
         b3_sb = held.tile([P, H3 // P], F32, name="b3_sb")

@@ -15,7 +15,7 @@ BANK = 512
 WIDTHS = (BANK,) * (N // BANK - 1) + (BANK // 2,) * 2
 STARTS = tuple(sum(WIDTHS[:n]) for n in range(len(WIDTHS)))
 CHUNKS = len(WIDTHS)
-WARM_UP = 2
+WARM_UP = 16
 MARGIN = 16
 
 FLOPS = 2 * N * (CTX * E * H1 + H1 * H2 + H2 * H3 + H3 * C)
@@ -29,11 +29,11 @@ def tile_contextualmlpdecryptor_b_kernel(tc, x, w1, b1, w2, b2, w3, b3, w4, b4, 
         tc.tile_pool(name="wide", bufs=2) as wide,
         tc.psum_pool(name="psum", bufs=8) as psum,
     ):
-        zeros = held.tile([P, BANK], BF16, name="zeros")
-        nc.vector.memset(zeros[:], 0.0)
+        zeros = held.tile([P, P], BF16, name="zeros")
+        nc.gpsimd.memset(zeros[:], 0.0)
         unread = psum.tile([P, BANK], F32, name="acc")
         for turn in range(WARM_UP):
-            nc.tensor.matmul(unread[:], zeros[:, 0:P], zeros[:], start=True, stop=True)
+            nc.tensor.matmul(unread[:, 0:P], zeros[:], zeros[:], start=True, stop=True)
 
         xp = held.tile([P, MARGIN + N + MARGIN], BF16, name="xp")
         nc.vector.memset(xp[:, 0:MARGIN], 0.0)

@@ -131,6 +131,10 @@ def tile_contextualmlpdecryptor_b_kernel(tc, x, w1, b1, w2, b2, w3, b3, w4, b4, 
                 b4_wide[:],
                 ADD,
             )
-            nc.sync.dma_start(out[c * P : (c + 1) * P, :], windows[c][:])
+            if c + 1 < C // P:
+                nc.sync.dma_start(out[c * P : (c + 1) * P, :], windows[c][:])
+            else:
+                for queue, half in ((nc.sync, slice(0, S // 2)), (nc.scalar, slice(S // 2, S))):
+                    queue.dma_start(out[c * P : (c + 1) * P, half], windows[c][:, half])
             if c + 1 < C // P:
                 b4_wide = widen_bias(c + 1)

@@ -16,6 +16,7 @@ WIDTHS = (BANK,) * (N // BANK - 1) + (BANK // 2,) * 2
 STARTS = tuple(sum(WIDTHS[:n]) for n in range(len(WIDTHS)))
 CHUNKS = len(WIDTHS)
 WARM_UP = 16
+LAST_PIECES = 4
 MARGIN = 16
 
 FLOPS = 2 * N * (CTX * E * H1 + H1 * H2 + H2 * H3 + H3 * C)
@@ -131,10 +132,10 @@ def tile_contextualmlpdecryptor_b_kernel(tc, x, w1, b1, w2, b2, w3, b3, w4, b4, 
                 b4_wide[:],
                 ADD,
             )
-            if c + 1 < C // P:
-                nc.sync.dma_start(out[c * P : (c + 1) * P, :], windows[c][:])
-            else:
-                for queue, half in ((nc.sync, slice(0, S // 2)), (nc.scalar, slice(S // 2, S))):
-                    queue.dma_start(out[c * P : (c + 1) * P, half], windows[c][:, half])
+            pieces = 1 if c + 1 < C // P else LAST_PIECES
+            for piece in range(pieces):
+                columns = slice(piece * S // pieces, (piece + 1) * S // pieces)
+                queue = nc.sync if piece % 2 == 0 else nc.scalar
+                queue.dma_start(out[c * P : (c + 1) * P, columns], windows[c][:, columns])
             if c + 1 < C // P:
                 b4_wide = widen_bias(c + 1)

@@ -15,7 +15,7 @@ BANK = 512
 WIDTHS = (BANK,) * (N // BANK - 1) + (BANK // 2,) * 2
 STARTS = tuple(sum(WIDTHS[:n]) for n in range(len(WIDTHS)))
 CHUNKS = len(WIDTHS)
-WARM_UP = 16
+WARM_UP = 12
 LAST_PIECES = 4
 MARGIN = 16
 

@@ -40,11 +40,16 @@ def tile_contextualmlpdecryptor_b_kernel(tc, x, w1, b1, w2, b2, w3, b3, w4, b4, 
         nc.vector.memset(xp[:, 0:MARGIN], 0.0)
         nc.vector.memset(xp[:, MARGIN + N : MARGIN + N + MARGIN], 0.0)
         w1_sb = held.tile([P, CTX, H1], BF16, name="w1_sb")
-        nc.sync.dma_start(xp[:, MARGIN : MARGIN + BANK], x[:, 0:BANK])
+        edges = [0] + [(n + 1) * BANK + MARGIN for n in range(N // BANK - 1)] + [N]
+
+        def load_x(n):
+            nc.sync.dma_start(xp[:, MARGIN + edges[n] : MARGIN + edges[n + 1]], x[:, edges[n] : edges[n + 1]])
+
+        load_x(0)
         for i in range(CTX):
             nc.sync.dma_start(w1_sb[:, i, :], w1[i * E : (i + 1) * E, :])
         for n in range(1, N // BANK):
-            nc.sync.dma_start(xp[:, MARGIN + n * BANK : MARGIN + (n + 1) * BANK], x[:, n * BANK : (n + 1) * BANK])
+            load_x(n)
         b1_sb = held.tile([P, H1 // P], F32, name="b1_sb")
         b2_sb = held.tile([P, H2 // P], F32, name="b2_sb")
         b3_sb = held.tile([P, H3 // P], F32, name="b3_sb")
@@ -80,17 +85,18 @@ def tile_contextualmlpdecryptor_b_kernel(tc, x, w1, b1, w2, b2, w3, b3, w4, b4, 
 
         h1 = [held.tile([P, H1 // P, WIDTHS[n]], BF16, name=f"h1_{n}") for n in range(CHUNKS)]
         for n in range(CHUNKS):
-            for m in range(H1 // P):
-                acc = psum.tile([P, BANK], F32, name="acc")
-                for i in range(CTX):
+            accs = [psum.tile([P, BANK], F32, name="acc") for m in range(H1 // P)]
+            for i in range(CTX):
+                for m in range(H1 // P):
                     nc.tensor.matmul(
-                        acc[:, 0 : WIDTHS[n]],
+                        accs[m][:, 0 : WIDTHS[n]],
                         w1_sb[:, i, m * P : (m + 1) * P],
                         xp[:, MARGIN - PAD + STARTS[n] + i : MARGIN - PAD + STARTS[n] + i + WIDTHS[n]],
                         start=(i == 0),
                         stop=(i == CTX - 1),
                     )
-                relu_bias(m, h1[n][:, m, :], acc[:, 0 : WIDTHS[n]], b1_sb[:, m : m + 1])
+            for m in range(H1 // P):
+                relu_bias(m, h1[n][:, m, :], accs[m][:, 0 : WIDTHS[n]], b1_sb[:, m : m + 1])
 
         h2 = [held.tile([P, H2 // P, WIDTHS[n]], BF16, name=f"h2_{n}") for n in range(CHUNKS)]
         for n in range(CHUNKS):

import concourse.mybir as mybir

F32 = mybir.dt.float32
BF16 = mybir.dt.bfloat16
U16 = mybir.dt.uint16
RELU = mybir.ActivationFunctionType.Relu
ADD = mybir.AluOpType.add
MAX = mybir.AluOpType.max

P = 128
E, CTX, PAD = 128, 5, 2
H1, H2, H3 = 512, 256, 128
C, S, N = 1024, 4096, 2048
BANK = 512
WIDTHS = (BANK,) * (N // BANK - 1) + (BANK // 2,) * 2
STARTS = tuple(sum(WIDTHS[:n]) for n in range(len(WIDTHS)))
CHUNKS = len(WIDTHS)
WARM_UP = 12
LAST_PIECES = 4
MARGIN = 16

FLOPS = 2 * N * (CTX * E * H1 + H1 * H2 + H2 * H3 + H3 * C)


def tile_contextualmlpdecryptor_b_kernel(tc, x, w1, b1, w2, b2, w3, b3, w4, b4, base, offs, out):
    nc = tc.nc
    with (
        tc.tile_pool(name="held", bufs=1) as held,
        tc.tile_pool(name="dense", bufs=3) as dense,
        tc.tile_pool(name="wide", bufs=2) as wide,
        tc.psum_pool(name="psum", bufs=8) as psum,
    ):
        zeros = held.tile([P, P], BF16, name="zeros")
        nc.gpsimd.memset(zeros[:], 0.0)
        unread = psum.tile([P, BANK], F32, name="acc")
        for turn in range(WARM_UP):
            nc.tensor.matmul(unread[:, 0:P], zeros[:], zeros[:], start=True, stop=True)

        xp = held.tile([P, MARGIN + N + MARGIN], BF16, name="xp")
        nc.vector.memset(xp[:, 0:MARGIN], 0.0)
        nc.vector.memset(xp[:, MARGIN + N : MARGIN + N + MARGIN], 0.0)
        w1_sb = held.tile([P, CTX, H1], BF16, name="w1_sb")
        edges = [0] + [(n + 1) * BANK + MARGIN for n in range(N // BANK - 1)] + [N]

        def load_x(n):
            nc.sync.dma_start(xp[:, MARGIN + edges[n] : MARGIN + edges[n + 1]], x[:, edges[n] : edges[n + 1]])

        load_x(0)
        for i in range(CTX):
            nc.sync.dma_start(w1_sb[:, i, :], w1[i * E : (i + 1) * E, :])
        for n in range(1, N // BANK):
            load_x(n)
        b1_sb = held.tile([P, H1 // P], F32, name="b1_sb")
        b2_sb = held.tile([P, H2 // P], F32, name="b2_sb")
        b3_sb = held.tile([P, H3 // P], F32, name="b3_sb")
        b4_sb = held.tile([P, C // P], F32, name="b4_sb")
        with nc.allow_non_contiguous_dma(reason="a bias has one 4-byte value for each partition"):
            for bias_sb, bias in ((b1_sb, b1), (b2_sb, b2), (b3_sb, b3), (b4_sb, b4)):
                nc.sync.dma_start(bias_sb[:], bias.rearrange("(m p) o -> p (m o)", p=P))
        w2_sb = held.tile([P, H1 // P, H2], BF16, name="w2_sb")
        nc.sync.dma_start(w2_sb[:], w2.rearrange("(k p) m -> p k m", p=P))
        w3_sb = held.tile([P, H2 // P, H3], BF16, name="w3_sb")
        nc.sync.dma_start(w3_sb[:], w3.rearrange("(k p) m -> p k m", p=P))
        w4_sb = held.tile([P, C], BF16, name="w4_sb")
        nc.sync.dma_start(w4_sb[:], w4)
        offsets = held.tile([P, N // 16], U16, name="offsets")
        nc.sync.dma_start(offsets[:], offs)

        windows = [held.tile([P, S], F32, name=f"window{c}") for c in range(C // P)]
        for c in range(C // P):
            nc.sync.dma_start(windows[c][:], base[c * P : (c + 1) * P, :])

        def widen_bias(c):
            b4_wide = wide.tile([P, N], F32, name="b4_wide")
            nc.scalar.copy(b4_wide[:], b4_sb[:, c : c + 1].to_broadcast([P, N]))
            return b4_wide

        b4_wide = widen_bias(0)

        def relu_bias(turn, out_ap, acc, bias_column):
            if turn % 2 == 0:
                nc.scalar.activation(out_ap, acc, RELU, bias=bias_column)
            else:
                nc.vector.tensor_scalar(out_ap, acc, bias_column, 0.0, ADD, MAX)

        h1 = [held.tile([P, H1 // P, WIDTHS[n]], BF16, name=f"h1_{n}") for n in range(CHUNKS)]
        for n in range(CHUNKS):
            accs = [psum.tile([P, BANK], F32, name="acc") for m in range(H1 // P)]
            for i in range(CTX):
                for m in range(H1 // P):
                    nc.tensor.matmul(
                        accs[m][:, 0 : WIDTHS[n]],
                        w1_sb[:, i, m * P : (m + 1) * P],
                        xp[:, MARGIN - PAD + STARTS[n] + i : MARGIN - PAD + STARTS[n] + i + WIDTHS[n]],
                        start=(i == 0),
                        stop=(i == CTX - 1),
                    )
            for m in range(H1 // P):
                relu_bias(m, h1[n][:, m, :], accs[m][:, 0 : WIDTHS[n]], b1_sb[:, m : m + 1])

        h2 = [held.tile([P, H2 // P, WIDTHS[n]], BF16, name=f"h2_{n}") for n in range(CHUNKS)]
        for n in range(CHUNKS):
            for m in range(H2 // P):
                acc = psum.tile([P, BANK], F32, name="acc")
                for k in range(H1 // P):
                    nc.tensor.matmul(
                        acc[:, 0 : WIDTHS[n]],
                        w2_sb[:, k, m * P : (m + 1) * P],
                        h1[n][:, k, :],
                        start=(k == 0),
                        stop=(k == H1 // P - 1),
                    )
                relu_bias(m, h2[n][:, m, :], acc[:, 0 : WIDTHS[n]], b2_sb[:, m : m + 1])

        h3 = [held.tile([P, WIDTHS[n]], BF16, name=f"h3_{n}") for n in range(CHUNKS)]
        for n in range(CHUNKS):
            acc = psum.tile([P, BANK], F32, name="acc")
            for k in range(H2 // P):
                nc.tensor.matmul(
                    acc[:, 0 : WIDTHS[n]], w3_sb[:, k, :], h2[n][:, k, :], start=(k == 0), stop=(k == H2 // P - 1)
                )
            relu_bias(n, h3[n][:], acc[:, 0 : WIDTHS[n]], b3_sb[:, 0:1])

        for c in range(C // P):
            product = dense.tile([P, N], F32, name="product")
            for n in range(CHUNKS):
                acc = psum.tile([P, BANK], F32, name="acc")
                nc.tensor.matmul(
                    acc[:, 0 : WIDTHS[n]], w4_sb[:, c * P : (c + 1) * P], h3[n][:], start=True, stop=True
                )
                if c == 0 and n % 2 == 1:
                    nc.vector.tensor_copy(product[:, STARTS[n] : STARTS[n] + WIDTHS[n]], acc[:, 0 : WIDTHS[n]])
                else:
                    nc.scalar.copy(product[:, STARTS[n] : STARTS[n] + WIDTHS[n]], acc[:, 0 : WIDTHS[n]])
            nc.vector.tensor_tensor(
                windows[c][:].indirect(offsets[:]),
                product[:],
                b4_wide[:],
                ADD,
            )
            pieces = 1 if c + 1 < C // P else LAST_PIECES
            for piece in range(pieces):
                columns = slice(piece * S // pieces, (piece + 1) * S // pieces)
                queue = nc.sync if piece % 2 == 0 else nc.scalar
                queue.dma_start(out[c * P : (c + 1) * P, columns], windows[c][:, columns])
            if c + 1 < C // P:
                b4_wide = widen_bias(c + 1)
